import numpy as np
import ml_dtypes


def mxq(x, axis, fmt="e4m3"):
    dtype, down = {"e4m3": (ml_dtypes.float8_e4m3fn, 7), "e5m2": (ml_dtypes.float8_e5m2, 14)}[fmt]
    v = np.moveaxis(np.asarray(x, np.float32).astype(ml_dtypes.bfloat16).astype(np.float64), axis, -1)
    blocks = v.reshape(v.shape[:-1] + (-1, 32))
    amax = np.abs(blocks).max(-1, keepdims=True)
    byte = np.maximum(np.where(amax > 0, np.frexp(amax)[1] - 1 + 127, 0) - down, 1)
    scale = np.exp2(byte - 127.0)
    codes = (blocks / scale).astype(np.float32).astype(dtype).astype(np.float64)
    return np.moveaxis((codes * scale).reshape(v.shape), -1, axis)


WIDE = False


def mx_kscale(k):
    if not WIDE:
        return np.ones(k)
    levels = np.array([10, -10, 5, -5, 0])
    if k % 512:
        return np.exp2(np.random.permutation(np.resize(levels, k // 32))).repeat(32)
    a = np.empty((k // 512, 16))
    for p in range(k // 512):
        a[p, :8] = np.random.permutation(np.resize(levels, 8))
        for g in range(8):
            far = levels[np.abs(levels - a[p, g]) >= 10]
            a[p, g + 8] = far[np.random.randint(len(far))]
    return np.exp2(a.ravel()).repeat(32)


BF16 = ml_dtypes.bfloat16


def bf(x):
    return np.asarray(x, np.float32).astype(BF16)


def f64(x):
    return np.asarray(x).astype(np.float64)


B, EN_MID, DE_MID = 1024, 2048, 4096
K1 = EN_MID // 2
K2 = DE_MID // 2


def setup_inputs():
    s = mx_kscale(K1)
    in_data = np.random.standard_normal((B, K1, 2)) * s[None, :, None]
    return {"in_data": bf(in_data.reshape(B, EN_MID)),
            "W": bf(np.random.standard_normal((DE_MID, K1)) / np.sqrt(K1) / s[None, :]),
            "bias": bf(np.random.standard_normal(DE_MID) * 0.25)}


def reference(in_data, W, bias):
    Bsz = in_data.shape[0]
    x_imag = f64(in_data).reshape(Bsz, K1, 2)[:, :, 1]
    tmp = mxq(x_imag, 1, "e4m3") @ mxq(f64(W), 1, "e4m3").T
    act = np.maximum(tmp + f64(bias), 0.0)
    out_r = act[:, :K2] - act[:, K2:]
    out = np.stack([out_r, np.zeros_like(out_r)], axis=2)
    return out.reshape(Bsz, DE_MID, 1)

@@ -1,0 +1,333 @@
+from contextlib import ExitStack
+
+import concourse.mybir as mybir
+from concourse.masks import make_identity
+
+F32 = mybir.dt.float32
+BF16 = mybir.dt.bfloat16
+U32 = mybir.dt.uint32
+U8 = mybir.dt.uint8
+FP8X4 = mybir.dt.float8_e4m3fn_x4
+ALU = mybir.AluOpType
+
+P = 128
+B = 1024
+K = 1024
+HALF = 2048
+N_J = 8
+FLOPS = 2 * B * K * 2 * HALF
+WG_BUFS = 10
+HEAD_ENGINES = ("scalar", "vector", "scalar", "vector")
+EARLY_JOBS = (0, 1, 2)
+
+
+def tile_middlelayer_kernel(tc, in_data, W, bias, out):
+    nc = tc.nc
+    out2d = out.rearrange("b j o -> b (j o)")
+    out_view = out2d.rearrange("(c bb p) w -> c p bb w", c=2, bb=4, p=P)
+
+    with ExitStack() as ctx:
+        const = ctx.enter_context(tc.tile_pool(name="const", bufs=1))
+        io = ctx.enter_context(tc.tile_pool(name="io", bufs=8))
+        wraw = ctx.enter_context(tc.tile_pool(name="wraw", bufs=1))
+        stage = ctx.enter_context(tc.tile_pool(name="stage", bufs=3))
+        codes = ctx.enter_context(tc.tile_pool(name="codes", bufs=1))
+        epi = ctx.enter_context(tc.tile_pool(name="epi", bufs=4))
+        psum = ctx.enter_context(tc.psum_pool(name="psum", bufs=1))
+        ctx.enter_context(tc.manual_schedule())
+
+        ident = const.tile([P, P], F32, name="ident")
+        make_identity(nc, ident[:])
+        zeros = const.tile([P, 256], BF16, name="zeros")
+        nc.vector.memset(zeros[:], 0.0)
+        bias_rows = const.tile([P, 256], F32, name="bias_rows")
+        nc.vector.memset(bias_rows[:], 0.0)
+
+        bias_raw = const.tile([16, 256], BF16, name="bias_raw")
+        nc.scalar.dma_start(out=bias_raw[:], in_=bias.rearrange("(r q) -> r q", q=256))
+
+        x_in = {}
+        w_in = {}
+
+        def load_x_pair(pair):
+            t = io.tile([P, 2, 2 * K], BF16, name="xin%d" % pair, tag="io")
+            for i in range(2):
+                bb = 2 * pair + i
+                nc.sync.dma_start(out=t[:, i, :], in_=in_data[bb * P : (bb + 1) * P, :])
+                x_in[bb] = t[:, i, :]
+
+        def w_tile(J, h):
+            if (J, h) not in w_in:
+                w_in[(J, h)] = wraw.tile([P, 2, K], BF16, name="w%d_%d" % (J, h))
+            return w_in[(J, h)]
+
+        def w_rows(J, h):
+            row0 = h * HALF + J * 256
+            return W[row0 : row0 + 256, :].rearrange("(n s) k -> n s k", s=2)
+
+        def load_w(J, h):
+            nc.sync.dma_start(out=w_tile(J, h)[:], in_=w_rows(J, h))
+
+        load_x_pair(0)
+        load_x_pair(1)
+        for J in (0, 1, 2):
+            for h in (1, 0):
+                load_w(J, h)
+        load_x_pair(2)
+        load_x_pair(3)
+        for J in range(3, N_J):
+            for h in (1, 0):
+                load_w(J, h)
+
+        bank_count = [0]
+
+        def next_bank():
+            i = bank_count[0] % 4
+            bank_count[0] += 1
+            return psum.tile([P, 512], F32, name="m%d" % i, tag="m%d" % i)
+
+        r_bank = []
+        for bb in range(4):
+            t = psum.tile([P, 512], F32, name="rb%d" % bb, tag="rb%d" % bb)
+            nc.tensor.matmul(
+                out=t[:, 256:512], lhsT=zeros[:, 0:P], rhs=zeros[:, 0:256], start=True, stop=True
+            )
+            r_bank.append(t)
+
+        nc.vector.tensor_copy(
+            out=bias_rows[0:16, :].rearrange("r (s n) -> r s n", s=2),
+            in_=bias_raw[0:16, :].rearrange("r (n s) -> r s n", s=2),
+        )
+        bias_t = next_bank()
+        for s in range(2):
+            nc.tensor.transpose(
+                bias_t[:, s * P : (s + 1) * P], bias_rows[:, s * P : (s + 1) * P], ident[:]
+            )
+        bias_sb = const.tile([P, 2, 16], F32, name="bias_sb")
+        neg_b1 = const.tile([P, 2, 8], F32, name="neg_b1")
+        delta = const.tile([P, 2, 8], F32, name="delta")
+        nc.scalar.copy(
+            out=bias_sb[:], in_=bias_t[:, 0:256].rearrange("p (s r) -> p s r", s=2)[:, :, 0:16]
+        )
+
+        def bias_scalars():
+            nc.vector.tensor_scalar(
+                out=neg_b1[:], in0=bias_sb[:, :, 0:8], scalar1=-1.0, scalar2=None, op0=ALU.mult
+            )
+            nc.vector.tensor_tensor(
+                out=delta[:], in0=bias_sb[:, :, 8:16], in1=bias_sb[:, :, 0:8], op=ALU.subtract
+            )
+
+        x_codes = codes.tile([P, 2, B], U32, name="x_codes", align_bytes=64)
+        x_scales = codes.tile([P, 2, B], U8, name="x_scales", align_bytes=64)
+        w_codes = {}
+        w_scales = {}
+        for J in range(N_J):
+            for h in range(2):
+                w_codes[(J, h)] = codes.tile([P, 512], U32, name="wc%d_%d" % (J, h), align_bytes=64)
+                w_scales[(J, h)] = codes.tile([P, 512], U8, name="ws%d_%d" % (J, h), align_bytes=64)
+
+        def copy_out(engine, dst, src):
+            if engine == "vector":
+                nc.vector.tensor_copy(out=dst, in_=src)
+            else:
+                nc.scalar.copy(out=dst, in_=src)
+
+        x_compact = {}
+        x_grouped = {}
+
+        def x_compaction(bb, engine):
+            t = stage.tile([P, K], BF16, name="xcmp", tag="xcmp", bufs=4)
+            src = x_in[bb].rearrange("p (k two) -> p k two", two=2)[:, :, 1]
+            if engine == "vector":
+                nc.vector.tensor_copy(out=t[:], in_=src)
+            else:
+                nc.gpsimd.tensor_scalar(
+                    out=t[:], in0=src, scalar1=1.0, scalar2=0.0,
+                    op0=ALU.mult, op1=ALU.add,
+                )
+            x_compact[bb] = t
+
+        def x_transposes(bb, engine="scalar"):
+            words = x_compact[bb][:].bitcast(F32)
+            bank = next_bank()
+            for q in range(4):
+                g, u = divmod(q, 2)
+                nc.tensor.transpose(
+                    bank[:, q * P : (q + 1) * P], words[:, 256 * g + u : 256 * (g + 1) : 2], ident[:]
+                )
+            g_tile = stage.tile([P, K], BF16, name="xg", tag="xg", align_bytes=64)
+            copy_out(
+                engine,
+                g_tile[:].bitcast(F32).rearrange("p (g b u) -> p g b u", g=2, u=2),
+                bank[:].rearrange("p (g u b) -> p g b u", g=2, u=2),
+            )
+            x_grouped[bb] = g_tile
+
+        def x_quantise(bb):
+            for g in range(2):
+                nc.vector.quantize_mx(
+                    out=x_codes[:, g, bb * P : (bb + 1) * P].bitcast(FP8X4),
+                    scales=x_scales[:, g, bb * P : (bb + 1) * P],
+                    in_=x_grouped[bb][:, g * 512 : (g + 1) * 512],
+                )
+
+        w_grouped = {}
+
+        def w_transposes(J, h, s, engine="scalar"):
+            words = w_in[(J, h)][:, s, :].bitcast(F32)
+            g_tile = stage.tile([P, K], BF16, name="wg", tag="wg", bufs=WG_BUFS, align_bytes=64)
+            bank = next_bank()
+            for q in range(4):
+                g, u = divmod(q, 2)
+                nc.tensor.transpose(bank[:, q * P : (q + 1) * P], words[:, 256 * g + u : 256 * (g + 1) : 2], ident[:])
+            copy_out(
+                engine,
+                g_tile[:].bitcast(F32).rearrange("p (g n u) -> p g n u", g=2, u=2),
+                bank[:].rearrange("p (g u n) -> p g n u", g=2, u=2),
+            )
+            w_grouped[(J, h, s)] = g_tile
+
+        def w_quantise(J, h, s):
+            nc.vector.quantize_mx(
+                out=w_codes[(J, h)][:, s * 256 : (s + 1) * 256].bitcast(FP8X4),
+                scales=w_scales[(J, h)][:, s * 256 : (s + 1) * 256],
+                in_=w_grouped[(J, h, s)][:],
+            )
+
+        def quantise(job):
+            if job[0] == "x":
+                x_quantise(job[1])
+            else:
+                w_quantise(job[1], job[2], job[3])
+
+        def mx(J, c, s, h):
+            acc = next_bank()
+            for g in range(2):
+                lo = s * 256 + g * P
+                nc.tensor.matmul_mx(
+                    out=acc[:],
+                    lhsT=w_codes[(J, h)][:, lo : lo + P].bitcast(FP8X4),
+                    lhsT_scale=w_scales[(J, h)][:, lo : lo + P],
+                    rhs=x_codes[:, g, c * 512 : (c + 1) * 512].bitcast(FP8X4),
+                    rhs_scale=x_scales[:, g, c * 512 : (c + 1) * 512],
+                    start=(g == 0),
+                    stop=(g == 1),
+                )
+            return acc
+
+        def fold_first(J, s, acc):
+            d2 = epi.tile([P, 512], F32, name="d2", tag="d2")
+            nc.vector.tensor_scalar(
+                out=d2[:], in0=acc[:],
+                scalar1=delta[:, s, J : J + 1], scalar2=neg_b1[:, s, J : J + 1],
+                op0=ALU.add, op1=ALU.max,
+            )
+            return d2
+
+        def fold_second(J, s, acc, d2):
+            r = epi.tile([P, 512], F32, name="r", tag="r")
+            nc.vector.scalar_tensor_tensor(
+                out=r[:], in0=acc[:], scalar=neg_b1[:, s, J : J + 1], in1=d2[:],
+                op0=ALU.max, op1=ALU.subtract,
+            )
+            return r
+
+        def r_transposes(r_tiles):
+            for bb in range(4):
+                for s in range(2):
+                    nc.tensor.transpose(
+                        r_bank[bb][:, s * P : (s + 1) * P],
+                        r_tiles[s][:, bb * P : (bb + 1) * P],
+                        ident[:],
+                    )
+
+        def copy_out_and_store(J, c, vector_blocks, split_store):
+            o = io.tile([P, 4, 512], F32, name="o", tag="io")
+            for bb in range(4):
+                copy_out(
+                    "vector" if bb in vector_blocks else "scalar",
+                    o[:, bb, :].rearrange("p (n s e) -> p n s e", s=2, e=2),
+                    r_bank[bb][:].rearrange("p (e s n) -> p n s e", e=2, s=2),
+                )
+                if split_store:
+                    nc.sync.dma_start(
+                        out=out_view[c][:, bb, J * 512 : (J + 1) * 512], in_=o[:, bb, :]
+                    )
+            if not split_store:
+                nc.sync.dma_start(out=out_view[c][:, :, J * 512 : (J + 1) * 512], in_=o[:])
+
+        x_compaction(0, "vector")
+        x_transposes(0)
+        x_compaction(1, "vector")
+        x_transposes(1)
+        x_compaction(2, "vector")
+        x_quantise(0)
+        x_transposes(2)
+        x_compaction(3, "vector")
+        x_quantise(1)
+        x_transposes(3)
+        x_quantise(2)
+        bias_scalars()
+        head_w = [(0, 1, 0), (0, 1, 1), (0, 0, 0), (0, 0, 1)]
+        for i, (J, h, s) in enumerate(head_w):
+            w_transposes(J, h, s, HEAD_ENGINES[i])
+            if i == 0:
+                x_quantise(3)
+            if i >= 1:
+                w_quantise(*head_w[i - 1])
+        w_quantise(*head_w[3])
+        for bb in range(4, 8):
+            x_compaction(bb, "gpsimd")
+
+        rounds = [(J, c) for c in range(2) for J in range(3)]
+        rounds += [(J, c) for J in range(3, N_J) for c in range(2)]
+        n_rounds = len(rounds)
+        halves = [(J, h, s) for J in range(3, N_J) for h in (1, 0) for s in range(2)]
+        w_after = {0: [(J, h, s) for J in (1, 2) for h in (1, 0) for s in range(2)]}
+        for i in range(2, 12):
+            w_after[i] = halves[2 * (i - 2) : 2 * (i - 1)]
+        x_after = {1: [4, 5], 2: [6, 7]}
+
+        jobs = []
+        folded = {}
+        for i in range(n_rounds + 1):
+            last = i == n_rounds - 1
+            if 2 <= i < n_rounds:
+                J, c = rounds[i - 2]
+                copy_out_and_store(J, c, vector_blocks=(), split_store=False)
+            if i < n_rounds:
+                J, c = rounds[i]
+                acc = {}
+                acc[(0, 1)] = mx(J, c, 0, 1)
+                acc[(1, 1)] = mx(J, c, 1, 1)
+                if last:
+                    r_transposes(folded[i - 1])
+                    J1, c1 = rounds[i - 1]
+                    copy_out_and_store(J1, c1, vector_blocks=(), split_store=False)
+                acc[(0, 0)] = mx(J, c, 0, 0)
+                acc[(1, 0)] = mx(J, c, 1, 0)
+                d20 = fold_first(J, 0, acc[(0, 1)])
+                d21 = fold_first(J, 1, acc[(1, 1)])
+                r0 = fold_second(J, 0, acc[(0, 0)], d20)
+                r1 = fold_second(J, 1, acc[(1, 0)], d21)
+                for job in jobs:
+                    quantise(job)
+                folded[i] = [r0, r1]
+                jobs = []
+                for k, (Jw, h, s) in enumerate(w_after.get(i, [])):
+                    w_transposes(Jw, h, s, "scalar")
+                    jobs.append(("w", Jw, h, s))
+                for bb in x_after.get(i, []):
+                    x_transposes(bb)
+                    jobs.append(("x", bb))
+                if i in EARLY_JOBS:
+                    for job in jobs:
+                        quantise(job)
+                    jobs = []
+            if i >= 1 and i < n_rounds - 1:
+                r_transposes(folded[i - 1])
+            if i == n_rounds:
+                r_transposes(folded[i - 1])
+                J, c = rounds[i - 1]
+                copy_out_and_store(J, c, vector_blocks=(1, 3), split_store=True)

@@ -29,7 +29,7 @@ def tile_middlelayer_kernel(tc, in_data, W, bias, out):
     with ExitStack() as ctx:
         const = ctx.enter_context(tc.tile_pool(name="const", bufs=1))
         io = ctx.enter_context(tc.tile_pool(name="io", bufs=8))
-        wraw = ctx.enter_context(tc.tile_pool(name="wraw", bufs=1))
+        wraw = ctx.enter_context(tc.tile_pool(name="wraw", bufs=12))
         stage = ctx.enter_context(tc.tile_pool(name="stage", bufs=3))
         codes = ctx.enter_context(tc.tile_pool(name="codes", bufs=1))
         epi = ctx.enter_context(tc.tile_pool(name="epi", bufs=4))
@@ -58,7 +58,7 @@ def tile_middlelayer_kernel(tc, in_data, W, bias, out):
 
         def w_tile(J, h):
             if (J, h) not in w_in:
-                w_in[(J, h)] = wraw.tile([P, 2, K], BF16, name="w%d_%d" % (J, h))
+                w_in[(J, h)] = wraw.tile([P, 2, K], BF16, name="w%d_%d" % (J, h), tag="wraw")
             return w_in[(J, h)]
 
         def w_rows(J, h):
@@ -138,23 +138,26 @@ def tile_middlelayer_kernel(tc, in_data, W, bias, out):
 
         def x_compaction(bb, engine):
             t = stage.tile([P, K], BF16, name="xcmp", tag="xcmp", bufs=4)
-            src = x_in[bb].rearrange("p (k two) -> p k two", two=2)[:, :, 1]
-            if engine == "vector":
-                nc.vector.tensor_copy(out=t[:], in_=src)
-            else:
-                nc.gpsimd.tensor_scalar(
-                    out=t[:], in0=src, scalar1=1.0, scalar2=0.0,
-                    op0=ALU.mult, op1=ALU.add,
-                )
+            for g in range(2):
+                dst = t[:, g * 512 : (g + 1) * 512].rearrange("p (u i e) -> p u i e", u=2, e=2)
+                src = x_in[bb][:, g * K : (g + 1) * K].rearrange(
+                    "p (i u e two) -> p u i e two", u=2, e=2, two=2
+                )[:, :, :, :, 1]
+                if engine == "vector":
+                    nc.vector.tensor_copy(out=dst, in_=src)
+                else:
+                    nc.gpsimd.tensor_scalar(
+                        out=dst, in0=src, scalar1=1.0, scalar2=0.0,
+                        op0=ALU.mult, op1=ALU.add,
+                    )
             x_compact[bb] = t
 
         def x_transposes(bb, engine="scalar"):
             words = x_compact[bb][:].bitcast(F32)
             bank = next_bank()
             for q in range(4):
-                g, u = divmod(q, 2)
                 nc.tensor.transpose(
-                    bank[:, q * P : (q + 1) * P], words[:, 256 * g + u : 256 * (g + 1) : 2], ident[:]
+                    bank[:, q * P : (q + 1) * P], words[:, q * P : (q + 1) * P], ident[:]
                 )
             g_tile = stage.tile([P, K], BF16, name="xg", tag="xg", align_bytes=64)
             copy_out(
@@ -172,15 +175,32 @@ def tile_middlelayer_kernel(tc, in_data, W, bias, out):
                     in_=x_grouped[bb][:, g * 512 : (g + 1) * 512],
                 )
 
+        w_ordered = {}
         w_grouped = {}
 
+        def w_order(J, h, s):
+            t = stage.tile([P, K], BF16, name="word", tag="word", bufs=4)
+            nc.vector.tensor_copy(
+                out=t[:].bitcast(F32).rearrange("p (g u i) -> p g u i", g=2, u=2),
+                in_=w_in[(J, h)][:, s, :].bitcast(F32).rearrange("p (g i u) -> p g u i", g=2, u=2),
+            )
+            w_ordered[(J, h, s)] = t
+
         def w_transposes(J, h, s, engine="scalar"):
-            words = w_in[(J, h)][:, s, :].bitcast(F32)
+            ordered = (J, h, s) in w_ordered
+            if ordered:
+                words = w_ordered[(J, h, s)][:].bitcast(F32)
+            else:
+                words = w_in[(J, h)][:, s, :].bitcast(F32)
             g_tile = stage.tile([P, K], BF16, name="wg", tag="wg", bufs=WG_BUFS, align_bytes=64)
             bank = next_bank()
             for q in range(4):
                 g, u = divmod(q, 2)
-                nc.tensor.transpose(bank[:, q * P : (q + 1) * P], words[:, 256 * g + u : 256 * (g + 1) : 2], ident[:])
+                if ordered:
+                    cols = slice(q * P, (q + 1) * P)
+                else:
+                    cols = slice(256 * g + u, 256 * (g + 1), 2)
+                nc.tensor.transpose(bank[:, q * P : (q + 1) * P], words[:, cols], ident[:])
             copy_out(
                 engine,
                 g_tile[:].bitcast(F32).rearrange("p (g n u) -> p g n u", g=2, u=2),
@@ -315,6 +335,9 @@ def tile_middlelayer_kernel(tc, in_data, W, bias, out):
                     quantise(job)
                 folded[i] = [r0, r1]
                 jobs = []
+                if i >= 1:
+                    for block in w_after.get(i + 1, []):
+                        w_order(*block)
                 for k, (Jw, h, s) in enumerate(w_after.get(i, [])):
                     w_transposes(Jw, h, s, "scalar")
                     jobs.append(("w", Jw, h, s))

@@ -17,14 +17,11 @@ HALF = 2048
 N_J = 8
 FLOPS = 2 * B * K * 2 * HALF
 WG_BUFS = 10
-HEAD_ENGINES = ("scalar", "vector", "scalar", "vector")
-EARLY_JOBS = (0, 1, 2)
 
 
 def tile_middlelayer_kernel(tc, in_data, W, bias, out):
     nc = tc.nc
     out2d = out.rearrange("b j o -> b (j o)")
-    out_view = out2d.rearrange("(c bb p) w -> c p bb w", c=2, bb=4, p=P)
 
     with ExitStack() as ctx:
         const = ctx.enter_context(tc.tile_pool(name="const", bufs=1))
@@ -38,7 +35,7 @@ def tile_middlelayer_kernel(tc, in_data, W, bias, out):
 
         ident = const.tile([P, P], F32, name="ident")
         make_identity(nc, ident[:])
-        zeros = const.tile([P, 256], BF16, name="zeros")
+        zeros = const.tile([P, 512], BF16, name="zeros")
         nc.vector.memset(zeros[:], 0.0)
         bias_rows = const.tile([P, 256], F32, name="bias_rows")
         nc.vector.memset(bias_rows[:], 0.0)
@@ -69,10 +66,13 @@ def tile_middlelayer_kernel(tc, in_data, W, bias, out):
             nc.sync.dma_start(out=w_tile(J, h)[:], in_=w_rows(J, h))
 
         load_x_pair(0)
+        for h in (1, 0):
+            load_w(0, h)
         load_x_pair(1)
-        for J in (0, 1, 2):
-            for h in (1, 0):
-                load_w(J, h)
+        for h in (1, 0):
+            load_w(1, h)
+        for h in (1, 0):
+            load_w(2, h)
         load_x_pair(2)
         load_x_pair(3)
         for J in range(3, N_J):
@@ -86,13 +86,33 @@ def tile_middlelayer_kernel(tc, in_data, W, bias, out):
             bank_count[0] += 1
             return psum.tile([P, 512], F32, name="m%d" % i, tag="m%d" % i)
 
+        def r_tile(bb):
+            return psum.tile([P, 512], F32, name="rb%d" % bb, tag="rb%d" % bb)
+
+        spare_count = [0]
+
+        def spare_bank():
+            i = spare_count[0] % 3
+            spare_count[0] += 1
+            return r_tile(i)
+
+        idle = r_tile(3)
+
+        def keep_busy(n):
+            for i in range(n):
+                nc.tensor.matmul(out=idle[:], lhsT=zeros[:, 0:P], rhs=zeros[:], start=True, stop=True)
+
         r_bank = []
-        for bb in range(4):
-            t = psum.tile([P, 512], F32, name="rb%d" % bb, tag="rb%d" % bb)
-            nc.tensor.matmul(
-                out=t[:, 256:512], lhsT=zeros[:, 0:P], rhs=zeros[:, 0:256], start=True, stop=True
-            )
-            r_bank.append(t)
+
+        def open_r_banks():
+            for bb in range(4):
+                t = r_tile(bb)
+                nc.tensor.matmul(
+                    out=t[:, 256:512], lhsT=zeros[:, 0:P], rhs=zeros[:, 0:256], start=True, stop=True
+                )
+                r_bank.append(t)
+
+        keep_busy(4)
 
         nc.vector.tensor_copy(
             out=bias_rows[0:16, :].rearrange("r (s n) -> r s n", s=2),
@@ -136,7 +156,7 @@ def tile_middlelayer_kernel(tc, in_data, W, bias, out):
         x_compact = {}
         x_grouped = {}
 
-        def x_compaction(bb, engine):
+        def x_compaction(bb, engine="vector"):
             t = stage.tile([P, K], BF16, name="xcmp", tag="xcmp", bufs=4)
             for g in range(2):
                 dst = t[:, g * 512 : (g + 1) * 512].rearrange("p (u i e) -> p u i e", u=2, e=2)
@@ -147,19 +167,18 @@ def tile_middlelayer_kernel(tc, in_data, W, bias, out):
                     nc.vector.tensor_copy(out=dst, in_=src)
                 else:
                     nc.gpsimd.tensor_scalar(
-                        out=dst, in0=src, scalar1=1.0, scalar2=0.0,
-                        op0=ALU.mult, op1=ALU.add,
+                        out=dst, in0=src, scalar1=1.0, scalar2=0.0, op0=ALU.mult, op1=ALU.add
                     )
             x_compact[bb] = t
 
-        def x_transposes(bb, engine="scalar"):
+        def x_transposes(bb, engine="scalar", bank_of=next_bank):
             words = x_compact[bb][:].bitcast(F32)
-            bank = next_bank()
+            bank = bank_of()
             for q in range(4):
                 nc.tensor.transpose(
                     bank[:, q * P : (q + 1) * P], words[:, q * P : (q + 1) * P], ident[:]
                 )
-            g_tile = stage.tile([P, K], BF16, name="xg", tag="xg", align_bytes=64)
+            g_tile = stage.tile([P, K], BF16, name="xg", tag="xg", bufs=4, align_bytes=64)
             copy_out(
                 engine,
                 g_tile[:].bitcast(F32).rearrange("p (g b u) -> p g b u", g=2, u=2),
@@ -186,14 +205,14 @@ def tile_middlelayer_kernel(tc, in_data, W, bias, out):
             )
             w_ordered[(J, h, s)] = t
 
-        def w_transposes(J, h, s, engine="scalar"):
+        def w_transposes(J, h, s, engine="scalar", bank_of=next_bank):
             ordered = (J, h, s) in w_ordered
             if ordered:
                 words = w_ordered[(J, h, s)][:].bitcast(F32)
             else:
                 words = w_in[(J, h)][:, s, :].bitcast(F32)
             g_tile = stage.tile([P, K], BF16, name="wg", tag="wg", bufs=WG_BUFS, align_bytes=64)
-            bank = next_bank()
+            bank = bank_of()
             for q in range(4):
                 g, u = divmod(q, 2)
                 if ordered:
@@ -215,46 +234,58 @@ def tile_middlelayer_kernel(tc, in_data, W, bias, out):
                 in_=w_grouped[(J, h, s)][:],
             )
 
-        def quantise(job):
-            if job[0] == "x":
-                x_quantise(job[1])
+        def prepare(block):
+            if block[0] == "x":
+                x_compaction(block[1])
             else:
-                w_quantise(job[1], job[2], job[3])
+                w_order(*block[1:])
 
-        def mx(J, c, s, h):
+        def transpose(block, engine="scalar", bank_of=next_bank):
+            if block[0] == "x":
+                x_transposes(block[1], engine, bank_of)
+            else:
+                w_transposes(*block[1:], engine, bank_of)
+
+        def quantise(block):
+            if block[0] == "x":
+                x_quantise(block[1])
+            else:
+                w_quantise(*block[1:])
+
+        def mx(J, b0, nb, s, h):
             acc = next_bank()
             for g in range(2):
                 lo = s * 256 + g * P
                 nc.tensor.matmul_mx(
-                    out=acc[:],
+                    out=acc[:, 0:nb],
                     lhsT=w_codes[(J, h)][:, lo : lo + P].bitcast(FP8X4),
                     lhsT_scale=w_scales[(J, h)][:, lo : lo + P],
-                    rhs=x_codes[:, g, c * 512 : (c + 1) * 512].bitcast(FP8X4),
-                    rhs_scale=x_scales[:, g, c * 512 : (c + 1) * 512],
+                    rhs=x_codes[:, g, b0 : b0 + nb].bitcast(FP8X4),
+                    rhs_scale=x_scales[:, g, b0 : b0 + nb],
                     start=(g == 0),
                     stop=(g == 1),
                 )
             return acc
 
-        def fold_first(J, s, acc):
+        def fold_first(J, nb, s, acc):
             d2 = epi.tile([P, 512], F32, name="d2", tag="d2")
             nc.vector.tensor_scalar(
-                out=d2[:], in0=acc[:],
+                out=d2[:, 0:nb], in0=acc[:, 0:nb],
                 scalar1=delta[:, s, J : J + 1], scalar2=neg_b1[:, s, J : J + 1],
                 op0=ALU.add, op1=ALU.max,
             )
             return d2
 
-        def fold_second(J, s, acc, d2):
+        def fold_second(J, nb, s, acc, d2):
             r = epi.tile([P, 512], F32, name="r", tag="r")
             nc.vector.scalar_tensor_tensor(
-                out=r[:], in0=acc[:], scalar=neg_b1[:, s, J : J + 1], in1=d2[:],
+                out=r[:, 0:nb], in0=acc[:, 0:nb], scalar=neg_b1[:, s, J : J + 1], in1=d2[:, 0:nb],
                 op0=ALU.max, op1=ALU.subtract,
             )
             return r
 
-        def r_transposes(r_tiles):
-            for bb in range(4):
+        def r_transposes(nb, r_tiles):
+            for bb in range(nb // P):
                 for s in range(2):
                     nc.tensor.transpose(
                         r_bank[bb][:, s * P : (s + 1) * P],
@@ -262,95 +293,108 @@ def tile_middlelayer_kernel(tc, in_data, W, bias, out):
                         ident[:],
                     )
 
-        def copy_out_and_store(J, c, vector_blocks, split_store):
+        def copy_out_and_store(J, b0, nb, vector_blocks, split_store):
+            n_bb = nb // P
             o = io.tile([P, 4, 512], F32, name="o", tag="io")
-            for bb in range(4):
+            view = out2d[b0 : b0 + nb, J * 512 : (J + 1) * 512].rearrange("(bb p) w -> p bb w", p=P)
+            for bb in range(n_bb):
                 copy_out(
                     "vector" if bb in vector_blocks else "scalar",
                     o[:, bb, :].rearrange("p (n s e) -> p n s e", s=2, e=2),
                     r_bank[bb][:].rearrange("p (e s n) -> p n s e", e=2, s=2),
                 )
                 if split_store:
-                    nc.sync.dma_start(
-                        out=out_view[c][:, bb, J * 512 : (J + 1) * 512], in_=o[:, bb, :]
-                    )
+                    nc.sync.dma_start(out=view[:, bb, :], in_=o[:, bb, :])
             if not split_store:
-                nc.sync.dma_start(out=out_view[c][:, :, J * 512 : (J + 1) * 512], in_=o[:])
+                nc.sync.dma_start(out=view, in_=o[:, 0:n_bb, :])
 
-        x_compaction(0, "vector")
-        x_transposes(0)
-        x_compaction(1, "vector")
-        x_transposes(1)
-        x_compaction(2, "vector")
-        x_quantise(0)
-        x_transposes(2)
-        x_compaction(3, "vector")
-        x_quantise(1)
-        x_transposes(3)
-        x_quantise(2)
-        bias_scalars()
-        head_w = [(0, 1, 0), (0, 1, 1), (0, 0, 0), (0, 0, 1)]
-        for i, (J, h, s) in enumerate(head_w):
-            w_transposes(J, h, s, HEAD_ENGINES[i])
-            if i == 0:
-                x_quantise(3)
-            if i >= 1:
-                w_quantise(*head_w[i - 1])
-        w_quantise(*head_w[3])
-        for bb in range(4, 8):
-            x_compaction(bb, "gpsimd")
-
-        rounds = [(J, c) for c in range(2) for J in range(3)]
-        rounds += [(J, c) for J in range(3, N_J) for c in range(2)]
+        rounds = [(0, 0, 256), (0, 256, 256), (1, 0, 512), (2, 0, 512)]
+        rounds += [(J, 512, 512) for J in range(3)]
+        rounds += [(J, b0, 512) for J in range(3, N_J) for b0 in (0, 512)]
+        J, b0, nb = rounds.pop()
+        rounds += [(J, b0, 256), (J, b0 + 256, 256)]
         n_rounds = len(rounds)
-        halves = [(J, h, s) for J in range(3, N_J) for h in (1, 0) for s in range(2)]
-        w_after = {0: [(J, h, s) for J in (1, 2) for h in (1, 0) for s in range(2)]}
-        for i in range(2, 12):
-            w_after[i] = halves[2 * (i - 2) : 2 * (i - 1)]
-        x_after = {1: [4, 5], 2: [6, 7]}
 
-        jobs = []
+        def w_blocks(J, h):
+            return [("w", J, h, s) for s in range(2)]
+
+        after = {
+            0: [("x", 2), ("x", 3)] + w_blocks(1, 1),
+            1: w_blocks(1, 0) + w_blocks(2, 1),
+            2: w_blocks(2, 0) + [("x", 4), ("x", 5)],
+            3: [("x", 6), ("x", 7)],
+        }
+        for J in range(3, N_J):
+            after[2 * J - 2] = w_blocks(J, 1)
+            after[2 * J - 1] = w_blocks(J, 0)
+
+        x_compaction(0)
+        x_transposes(0, "scalar", spare_bank)
+        x_compaction(1)
+        keep_busy(1)
+        x_transposes(1, "scalar", spare_bank)
+        for block in w_blocks(0, 1):
+            prepare(block)
+            transpose(block, "scalar", spare_bank)
+        x_quantise(0)
+        x_quantise(1)
+        for block in w_blocks(0, 0):
+            prepare(block)
+            keep_busy(1)
+            transpose(block, "scalar", spare_bank)
+        for block in w_blocks(0, 1):
+            quantise(block)
+        bias_scalars()
+        x_compaction(2)
+        for block in w_blocks(0, 0):
+            quantise(block)
+
+        waiting = []
         folded = {}
-        for i in range(n_rounds + 1):
+        for i in range(n_rounds):
+            J, b0, nb = rounds[i]
             last = i == n_rounds - 1
-            if 2 <= i < n_rounds:
-                J, c = rounds[i - 2]
-                copy_out_and_store(J, c, vector_blocks=(), split_store=False)
-            if i < n_rounds:
-                J, c = rounds[i]
-                acc = {}
-                acc[(0, 1)] = mx(J, c, 0, 1)
-                acc[(1, 1)] = mx(J, c, 1, 1)
-                if last:
-                    r_transposes(folded[i - 1])
-                    J1, c1 = rounds[i - 1]
-                    copy_out_and_store(J1, c1, vector_blocks=(), split_store=False)
-                acc[(0, 0)] = mx(J, c, 0, 0)
-                acc[(1, 0)] = mx(J, c, 1, 0)
-                d20 = fold_first(J, 0, acc[(0, 1)])
-                d21 = fold_first(J, 1, acc[(1, 1)])
-                r0 = fold_second(J, 0, acc[(0, 0)], d20)
-                r1 = fold_second(J, 1, acc[(1, 0)], d21)
-                for job in jobs:
-                    quantise(job)
-                folded[i] = [r0, r1]
-                jobs = []
-                if i >= 1:
-                    for block in w_after.get(i + 1, []):
-                        w_order(*block)
-                for k, (Jw, h, s) in enumerate(w_after.get(i, [])):
-                    w_transposes(Jw, h, s, "scalar")
-                    jobs.append(("w", Jw, h, s))
-                for bb in x_after.get(i, []):
-                    x_transposes(bb)
-                    jobs.append(("x", bb))
-                if i in EARLY_JOBS:
-                    for job in jobs:
-                        quantise(job)
-                    jobs = []
-            if i >= 1 and i < n_rounds - 1:
-                r_transposes(folded[i - 1])
-            if i == n_rounds:
-                r_transposes(folded[i - 1])
-                J, c = rounds[i - 1]
-                copy_out_and_store(J, c, vector_blocks=(1, 3), split_store=True)
+            if i >= 2:
+                copy_out_and_store(*rounds[i - 2], vector_blocks=(), split_store=False)
+            acc = {}
+            acc[(0, 1)] = mx(J, b0, nb, 0, 1)
+            acc[(1, 1)] = mx(J, b0, nb, 1, 1)
+            if last:
+                r_transposes(rounds[i - 1][2], folded[i - 1])
+                copy_out_and_store(*rounds[i - 1], vector_blocks=(), split_store=False)
+            acc[(0, 0)] = mx(J, b0, nb, 0, 0)
+            acc[(1, 0)] = mx(J, b0, nb, 1, 0)
+            d20 = fold_first(J, nb, 0, acc[(0, 1)])
+            d21 = fold_first(J, nb, 1, acc[(1, 1)])
+            if i == 0:
+                x_compaction(3)
+                for bb in range(4, 8):
+                    x_compaction(bb, "gpsimd")
+            r0 = fold_second(J, nb, 0, acc[(0, 0)], d20)
+            r1 = fold_second(J, nb, 1, acc[(1, 0)], d21)
+            folded[i] = [r0, r1]
+            for block in waiting:
+                quantise(block)
+            waiting = []
+            for block in after.get(i, []):
+                transpose(block, "scalar", spare_bank if i == 0 or block[0:3] == ("w", 1, 0) else next_bank)
+            if i == 0:
+                keep_busy(1)
+            if i == 1:
+                open_r_banks()
+            if i >= 1 and not last:
+                r_transposes(rounds[i - 1][2], folded[i - 1])
+            ahead = [block for block in after.get(i + 1, []) if block[0] == "w" and block[1] >= 2]
+            if i >= 4:
+                for block in ahead:
+                    prepare(block)
+            if i < 4:
+                for block in after.get(i, []):
+                    quantise(block)
+            else:
+                waiting = after.get(i, [])
+            if i < 4:
+                for block in ahead:
+                    prepare(block)
+        r_transposes(rounds[n_rounds - 1][2], folded[n_rounds - 1])
+        copy_out_and_store(*rounds[n_rounds - 1], vector_blocks=(1,), split_store=True)

@@ -293,7 +293,7 @@ def tile_middlelayer_kernel(tc, in_data, W, bias, out):
                         ident[:],
                     )
 
-        def copy_out_and_store(J, b0, nb, vector_blocks, split_store):
+        def copy_out_and_store(J, b0, nb, vector_blocks, per_store):
             n_bb = nb // P
             o = io.tile([P, 4, 512], F32, name="o", tag="io")
             view = out2d[b0 : b0 + nb, J * 512 : (J + 1) * 512].rearrange("(bb p) w -> p bb w", p=P)
@@ -303,10 +303,9 @@ def tile_middlelayer_kernel(tc, in_data, W, bias, out):
                     o[:, bb, :].rearrange("p (n s e) -> p n s e", s=2, e=2),
                     r_bank[bb][:].rearrange("p (e s n) -> p n s e", e=2, s=2),
                 )
-                if split_store:
-                    nc.sync.dma_start(out=view[:, bb, :], in_=o[:, bb, :])
-            if not split_store:
-                nc.sync.dma_start(out=view, in_=o[:, 0:n_bb, :])
+                if bb % per_store == per_store - 1:
+                    lo = bb + 1 - per_store
+                    nc.sync.dma_start(out=view[:, lo : bb + 1, :], in_=o[:, lo : bb + 1, :])
 
         rounds = [(0, 0, 256), (0, 256, 256), (1, 0, 512), (2, 0, 512)]
         rounds += [(J, 512, 512) for J in range(3)]
@@ -355,13 +354,13 @@ def tile_middlelayer_kernel(tc, in_data, W, bias, out):
             J, b0, nb = rounds[i]
             last = i == n_rounds - 1
             if i >= 2:
-                copy_out_and_store(*rounds[i - 2], vector_blocks=(), split_store=False)
+                copy_out_and_store(*rounds[i - 2], vector_blocks=(), per_store=2 if i < n_rounds - 4 else 1)
             acc = {}
             acc[(0, 1)] = mx(J, b0, nb, 0, 1)
             acc[(1, 1)] = mx(J, b0, nb, 1, 1)
             if last:
                 r_transposes(rounds[i - 1][2], folded[i - 1])
-                copy_out_and_store(*rounds[i - 1], vector_blocks=(), split_store=False)
+                copy_out_and_store(*rounds[i - 1], vector_blocks=(), per_store=1)
             acc[(0, 0)] = mx(J, b0, nb, 0, 0)
             acc[(1, 0)] = mx(J, b0, nb, 1, 0)
             d20 = fold_first(J, nb, 0, acc[(0, 1)])
@@ -397,4 +396,4 @@ def tile_middlelayer_kernel(tc, in_data, W, bias, out):
                 for block in ahead:
                     prepare(block)
         r_transposes(rounds[n_rounds - 1][2], folded[n_rounds - 1])
-        copy_out_and_store(*rounds[n_rounds - 1], vector_blocks=(1,), split_store=True)
+        copy_out_and_store(*rounds[n_rounds - 1], vector_blocks=(1,), per_store=1)

@@ -86,33 +86,42 @@ def tile_middlelayer_kernel(tc, in_data, W, bias, out):
             bank_count[0] += 1
             return psum.tile([P, 512], F32, name="m%d" % i, tag="m%d" % i)
 
-        def r_tile(bb):
-            return psum.tile([P, 512], F32, name="rb%d" % bb, tag="rb%d" % bb)
+        r_bank = []
+        for bb in range(4):
+            t = psum.tile([P, 512], F32, name="rb%d" % bb, tag="rb%d" % bb)
+            nc.tensor.matmul(
+                out=t[:, 256:512], lhsT=zeros[:, 0:P], rhs=zeros[:, 0:256], start=True, stop=True
+            )
+            r_bank.append(t)
 
-        spare_count = [0]
-
-        def spare_bank():
-            i = spare_count[0] % 3
-            spare_count[0] += 1
-            return r_tile(i)
-
-        idle = r_tile(3)
+        idle = psum.tile([P, 512], F32, name="m3", tag="m3")
 
         def keep_busy(n):
             for i in range(n):
                 nc.tensor.matmul(out=idle[:], lhsT=zeros[:, 0:P], rhs=zeros[:], start=True, stop=True)
 
-        r_bank = []
+        spare_count = [0]
 
-        def open_r_banks():
-            for bb in range(4):
-                t = r_tile(bb)
-                nc.tensor.matmul(
-                    out=t[:, 256:512], lhsT=zeros[:, 0:P], rhs=zeros[:, 0:256], start=True, stop=True
+        def spare_halves():
+            i = spare_count[0] % 4
+            spare_count[0] += 2
+            return [r_bank[i][:, 0:256], r_bank[i + 1][:, 0:256]]
+
+        def regroup(g_tile, bank, halves):
+            words = g_tile[:].bitcast(F32)
+            if bank is None:
+                for g in range(2):
+                    nc.scalar.copy(
+                        out=words[:, g * 256 : (g + 1) * 256].rearrange("p (b u) -> p b u", u=2),
+                        in_=halves[g].rearrange("p (u b) -> p b u", u=2),
+                    )
+            else:
+                nc.scalar.copy(
+                    out=words.rearrange("p (g b u) -> p g b u", g=2, u=2),
+                    in_=bank[:].rearrange("p (g u b) -> p g b u", g=2, u=2),
                 )
-                r_bank.append(t)
 
-        keep_busy(4)
+        keep_busy(2)
 
         nc.vector.tensor_copy(
             out=bias_rows[0:16, :].rearrange("r (s n) -> r s n", s=2),
@@ -156,7 +165,7 @@ def tile_middlelayer_kernel(tc, in_data, W, bias, out):
         x_compact = {}
         x_grouped = {}
 
-        def x_compaction(bb, engine="vector"):
+        def x_compaction(bb, engine):
             t = stage.tile([P, K], BF16, name="xcmp", tag="xcmp", bufs=4)
             for g in range(2):
                 dst = t[:, g * 512 : (g + 1) * 512].rearrange("p (u i e) -> p u i e", u=2, e=2)
@@ -165,25 +174,26 @@ def tile_middlelayer_kernel(tc, in_data, W, bias, out):
                 )[:, :, :, :, 1]
                 if engine == "vector":
                     nc.vector.tensor_copy(out=dst, in_=src)
+                elif engine == "scalar":
+                    nc.scalar.copy(out=dst, in_=src)
                 else:
                     nc.gpsimd.tensor_scalar(
                         out=dst, in0=src, scalar1=1.0, scalar2=0.0, op0=ALU.mult, op1=ALU.add
                     )
             x_compact[bb] = t
 
-        def x_transposes(bb, engine="scalar", bank_of=next_bank):
+        def x_transposes(bb, spare=False):
             words = x_compact[bb][:].bitcast(F32)
-            bank = bank_of()
-            for q in range(4):
-                nc.tensor.transpose(
-                    bank[:, q * P : (q + 1) * P], words[:, q * P : (q + 1) * P], ident[:]
-                )
+            bank = None if spare else next_bank()
+            halves = spare_halves() if spare else [bank[:, 0:256], bank[:, 256:512]]
+            for g in range(2):
+                for u in range(2):
+                    lo = g * 256 + u * P
+                    nc.tensor.transpose(
+                        halves[g][:, u * P : (u + 1) * P], words[:, lo : lo + P], ident[:]
+                    )
             g_tile = stage.tile([P, K], BF16, name="xg", tag="xg", bufs=4, align_bytes=64)
-            copy_out(
-                engine,
-                g_tile[:].bitcast(F32).rearrange("p (g b u) -> p g b u", g=2, u=2),
-                bank[:].rearrange("p (g u b) -> p g b u", g=2, u=2),
-            )
+            regroup(g_tile, bank, halves)
             x_grouped[bb] = g_tile
 
         def x_quantise(bb):
@@ -197,34 +207,27 @@ def tile_middlelayer_kernel(tc, in_data, W, bias, out):
         w_ordered = {}
         w_grouped = {}
 
-        def w_order(J, h, s):
-            t = stage.tile([P, K], BF16, name="word", tag="word", bufs=4)
-            nc.vector.tensor_copy(
-                out=t[:].bitcast(F32).rearrange("p (g u i) -> p g u i", g=2, u=2),
-                in_=w_in[(J, h)][:, s, :].bitcast(F32).rearrange("p (g i u) -> p g u i", g=2, u=2),
+        def w_order(J, h, s, engine="vector"):
+            t = stage.tile([P, K], BF16, name="word", tag="word", bufs=5)
+            copy_out(
+                engine,
+                t[:].bitcast(F32).rearrange("p (g u i) -> p g u i", g=2, u=2),
+                w_in[(J, h)][:, s, :].bitcast(F32).rearrange("p (g i u) -> p g u i", g=2, u=2),
             )
             w_ordered[(J, h, s)] = t
 
-        def w_transposes(J, h, s, engine="scalar", bank_of=next_bank):
-            ordered = (J, h, s) in w_ordered
-            if ordered:
-                words = w_ordered[(J, h, s)][:].bitcast(F32)
-            else:
-                words = w_in[(J, h)][:, s, :].bitcast(F32)
+        def w_transposes(J, h, s, spare=False):
+            words = w_ordered[(J, h, s)][:].bitcast(F32)
+            bank = None if spare else next_bank()
+            halves = spare_halves() if spare else [bank[:, 0:256], bank[:, 256:512]]
+            for g in range(2):
+                for u in range(2):
+                    lo = g * 256 + u * P
+                    nc.tensor.transpose(
+                        halves[g][:, u * P : (u + 1) * P], words[:, lo : lo + P], ident[:]
+                    )
             g_tile = stage.tile([P, K], BF16, name="wg", tag="wg", bufs=WG_BUFS, align_bytes=64)
-            bank = bank_of()
-            for q in range(4):
-                g, u = divmod(q, 2)
-                if ordered:
-                    cols = slice(q * P, (q + 1) * P)
-                else:
-                    cols = slice(256 * g + u, 256 * (g + 1), 2)
-                nc.tensor.transpose(bank[:, q * P : (q + 1) * P], words[:, cols], ident[:])
-            copy_out(
-                engine,
-                g_tile[:].bitcast(F32).rearrange("p (g n u) -> p g n u", g=2, u=2),
-                bank[:].rearrange("p (g u n) -> p g n u", g=2, u=2),
-            )
+            regroup(g_tile, bank, halves)
             w_grouped[(J, h, s)] = g_tile
 
         def w_quantise(J, h, s):
@@ -234,17 +237,14 @@ def tile_middlelayer_kernel(tc, in_data, W, bias, out):
                 in_=w_grouped[(J, h, s)][:],
             )
 
-        def prepare(block):
-            if block[0] == "x":
-                x_compaction(block[1])
-            else:
-                w_order(*block[1:])
+        def prepare(block, engine="vector"):
+            w_order(*block[1:], engine)
 
-        def transpose(block, engine="scalar", bank_of=next_bank):
+        def transpose(block, spare=False):
             if block[0] == "x":
-                x_transposes(block[1], engine, bank_of)
+                x_transposes(block[1], spare)
             else:
-                w_transposes(*block[1:], engine, bank_of)
+                w_transposes(*block[1:], spare)
 
         def quantise(block):
             if block[0] == "x":
@@ -252,20 +252,19 @@ def tile_middlelayer_kernel(tc, in_data, W, bias, out):
             else:
                 w_quantise(*block[1:])
 
-        def mx(J, b0, nb, s, h):
-            acc = next_bank()
+        def mx(acc, J, s, h, b0, first, n):
             for g in range(2):
                 lo = s * 256 + g * P
+                b = slice(b0 + first, b0 + first + n)
                 nc.tensor.matmul_mx(
-                    out=acc[:, 0:nb],
+                    out=acc[:, first : first + n],
                     lhsT=w_codes[(J, h)][:, lo : lo + P].bitcast(FP8X4),
                     lhsT_scale=w_scales[(J, h)][:, lo : lo + P],
-                    rhs=x_codes[:, g, b0 : b0 + nb].bitcast(FP8X4),
-                    rhs_scale=x_scales[:, g, b0 : b0 + nb],
+                    rhs=x_codes[:, g, b].bitcast(FP8X4),
+                    rhs_scale=x_scales[:, g, b],
                     start=(g == 0),
                     stop=(g == 1),
                 )
-            return acc
 
         def fold_first(J, nb, s, acc):
             d2 = epi.tile([P, 512], F32, name="d2", tag="d2")
@@ -284,11 +283,11 @@ def tile_middlelayer_kernel(tc, in_data, W, bias, out):
             )
             return r
 
-        def r_transposes(nb, r_tiles):
+        def r_transposes(b0, nb, r_tiles):
             for bb in range(nb // P):
                 for s in range(2):
                     nc.tensor.transpose(
-                        r_bank[bb][:, s * P : (s + 1) * P],
+                        r_bank[(b0 // P + bb) % 4][:, s * P : (s + 1) * P],
                         r_tiles[s][:, bb * P : (bb + 1) * P],
                         ident[:],
                     )
@@ -301,7 +300,7 @@ def tile_middlelayer_kernel(tc, in_data, W, bias, out):
                 copy_out(
                     "vector" if bb in vector_blocks else "scalar",
                     o[:, bb, :].rearrange("p (n s e) -> p n s e", s=2, e=2),
-                    r_bank[bb][:].rearrange("p (e s n) -> p n s e", e=2, s=2),
+                    r_bank[(b0 // P + bb) % 4][:].rearrange("p (e s n) -> p n s e", e=2, s=2),
                 )
                 if bb % per_store == per_store - 1:
                     lo = bb + 1 - per_store
@@ -327,24 +326,23 @@ def tile_middlelayer_kernel(tc, in_data, W, bias, out):
             after[2 * J - 2] = w_blocks(J, 1)
             after[2 * J - 1] = w_blocks(J, 0)
 
-        x_compaction(0)
-        x_transposes(0, "scalar", spare_bank)
-        x_compaction(1)
+        x_compaction(0, "vector")
+        x_transposes(0, True)
+        x_compaction(1, "vector")
         keep_busy(1)
-        x_transposes(1, "scalar", spare_bank)
+        x_transposes(1, True)
         for block in w_blocks(0, 1):
             prepare(block)
-            transpose(block, "scalar", spare_bank)
+            transpose(block, True)
         x_quantise(0)
         x_quantise(1)
         for block in w_blocks(0, 0):
             prepare(block)
-            keep_busy(1)
-            transpose(block, "scalar", spare_bank)
+            transpose(block, True)
         for block in w_blocks(0, 1):
             quantise(block)
         bias_scalars()
-        x_compaction(2)
+        x_compaction(2, "vector")
         for block in w_blocks(0, 0):
             quantise(block)
 
@@ -354,21 +352,24 @@ def tile_middlelayer_kernel(tc, in_data, W, bias, out):
             J, b0, nb = rounds[i]
             last = i == n_rounds - 1
             if i >= 2:
-                copy_out_and_store(*rounds[i - 2], vector_blocks=(), per_store=2 if i < n_rounds - 4 else 1)
+                copy_out_and_store(
+                    *rounds[i - 2], vector_blocks=(), per_store=2 if i < n_rounds - 4 else 1
+                )
             acc = {}
-            acc[(0, 1)] = mx(J, b0, nb, 0, 1)
-            acc[(1, 1)] = mx(J, b0, nb, 1, 1)
-            if last:
-                r_transposes(rounds[i - 1][2], folded[i - 1])
-                copy_out_and_store(*rounds[i - 1], vector_blocks=(), per_store=1)
-            acc[(0, 0)] = mx(J, b0, nb, 0, 0)
-            acc[(1, 0)] = mx(J, b0, nb, 1, 0)
+            for h in (1, 0):
+                for s in range(2):
+                    acc[(s, h)] = next_bank()
+            width = 256 if i == 4 else nb
+            for first in range(0, nb, width):
+                for h in (1, 0):
+                    for s in range(2):
+                        mx(acc[(s, h)], J, s, h, b0, first, width)
             d20 = fold_first(J, nb, 0, acc[(0, 1)])
             d21 = fold_first(J, nb, 1, acc[(1, 1)])
             if i == 0:
-                x_compaction(3)
-                for bb in range(4, 8):
-                    x_compaction(bb, "gpsimd")
+                x_compaction(3, "vector")
+                for block in w_blocks(1, 1):
+                    prepare(block, "scalar")
             r0 = fold_second(J, nb, 0, acc[(0, 0)], d20)
             r1 = fold_second(J, nb, 1, acc[(1, 0)], d21)
             folded[i] = [r0, r1]
@@ -376,24 +377,28 @@ def tile_middlelayer_kernel(tc, in_data, W, bias, out):
                 quantise(block)
             waiting = []
             for block in after.get(i, []):
-                transpose(block, "scalar", spare_bank if i == 0 or block[0:3] == ("w", 1, 0) else next_bank)
+                transpose(block, i == 0 or block[0:3] == ("w", 1, 0))
             if i == 0:
-                keep_busy(1)
-            if i == 1:
-                open_r_banks()
-            if i >= 1 and not last:
-                r_transposes(rounds[i - 1][2], folded[i - 1])
+                for block in w_blocks(1, 0):
+                    prepare(block, "scalar")
+            if i >= 1:
+                r_transposes(*rounds[i - 1][1:3], folded[i - 1])
             ahead = [block for block in after.get(i + 1, []) if block[0] == "w" and block[1] >= 2]
+            if i == 1:
+                x_compaction(4, "scalar")
+                x_compaction(5, "vector")
+            if i == 2:
+                x_compaction(6, "scalar")
+                x_compaction(7, "vector")
             if i >= 4:
                 for block in ahead:
                     prepare(block)
-            if i < 4:
+                waiting = after.get(i, [])
+            else:
                 for block in after.get(i, []):
                     quantise(block)
-            else:
-                waiting = after.get(i, [])
-            if i < 4:
                 for block in ahead:
                     prepare(block)
-        r_transposes(rounds[n_rounds - 1][2], folded[n_rounds - 1])
+        copy_out_and_store(*rounds[n_rounds - 2], vector_blocks=(1,), per_store=1)
+        r_transposes(*rounds[n_rounds - 1][1:3], folded[n_rounds - 1])
         copy_out_and_store(*rounds[n_rounds - 1], vector_blocks=(1,), per_store=1)

@@ -147,14 +147,14 @@ def tile_middlelayer_kernel(tc, in_data, W, bias, out):
                 out=delta[:], in0=bias_sb[:, :, 8:16], in1=bias_sb[:, :, 0:8], op=ALU.subtract
             )
 
-        x_codes = codes.tile([P, 2, B], U32, name="x_codes", align_bytes=64)
-        x_scales = codes.tile([P, 2, B], U8, name="x_scales", align_bytes=64)
+        x_codes = codes.tile([P, 2, B], U32, name="x_codes", align_bytes=256)
+        x_scales = codes.tile([P, 2, B], U8, name="x_scales", align_bytes=256)
         w_codes = {}
         w_scales = {}
         for J in range(N_J):
             for h in range(2):
-                w_codes[(J, h)] = codes.tile([P, 512], U32, name="wc%d_%d" % (J, h), align_bytes=64)
-                w_scales[(J, h)] = codes.tile([P, 512], U8, name="ws%d_%d" % (J, h), align_bytes=64)
+                w_codes[(J, h)] = codes.tile([P, 512], U32, name="wc%d_%d" % (J, h), align_bytes=256)
+                w_scales[(J, h)] = codes.tile([P, 512], U8, name="ws%d_%d" % (J, h), align_bytes=256)
 
         def copy_out(engine, dst, src):
             if engine == "vector":
@@ -353,15 +353,17 @@ def tile_middlelayer_kernel(tc, in_data, W, bias, out):
             last = i == n_rounds - 1
             if i >= 2:
                 copy_out_and_store(
-                    *rounds[i - 2], vector_blocks=(), per_store=2 if i < n_rounds - 4 else 1
+                    *rounds[i - 2],
+                    vector_blocks=(3,) if i == n_rounds - 2 else (),
+                    per_store=2 if i < n_rounds - 4 else 1,
                 )
             acc = {}
             for h in (1, 0):
                 for s in range(2):
                     acc[(s, h)] = next_bank()
-            width = 256 if i == 4 else nb
-            for first in range(0, nb, width):
-                for h in (1, 0):
+            for h in (1, 0):
+                width = 256 if i == 4 and h == 1 else nb
+                for first in range(0, nb, width):
                     for s in range(2):
                         mx(acc[(s, h)], J, s, h, b0, first, width)
             d20 = fold_first(J, nb, 0, acc[(0, 1)])
@@ -396,7 +398,10 @@ def tile_middlelayer_kernel(tc, in_data, W, bias, out):
                 waiting = after.get(i, [])
             else:
                 for block in after.get(i, []):
-                    quantise(block)
+                    if block[0:3] in (("w", 2, 1), ("w", 1, 1)):
+                        waiting.append(block)
+                    else:
+                        quantise(block)
                 for block in ahead:
                     prepare(block)
         copy_out_and_store(*rounds[n_rounds - 2], vector_blocks=(1,), per_store=1)

from contextlib import ExitStack

import concourse.mybir as mybir
from concourse.masks import make_identity

F32 = mybir.dt.float32
BF16 = mybir.dt.bfloat16
U32 = mybir.dt.uint32
U8 = mybir.dt.uint8
FP8X4 = mybir.dt.float8_e4m3fn_x4
ALU = mybir.AluOpType

P = 128
B = 1024
K = 1024
HALF = 2048
N_J = 8
FLOPS = 2 * B * K * 2 * HALF
WG_BUFS = 10


def tile_middlelayer_kernel(tc, in_data, W, bias, out):
    nc = tc.nc
    out2d = out.rearrange("b j o -> b (j o)")

    with ExitStack() as ctx:
        const = ctx.enter_context(tc.tile_pool(name="const", bufs=1))
        io = ctx.enter_context(tc.tile_pool(name="io", bufs=8))
        wraw = ctx.enter_context(tc.tile_pool(name="wraw", bufs=12))
        stage = ctx.enter_context(tc.tile_pool(name="stage", bufs=3))
        codes = ctx.enter_context(tc.tile_pool(name="codes", bufs=1))
        epi = ctx.enter_context(tc.tile_pool(name="epi", bufs=4))
        psum = ctx.enter_context(tc.psum_pool(name="psum", bufs=1))
        ctx.enter_context(tc.manual_schedule())

        ident = const.tile([P, P], F32, name="ident")
        make_identity(nc, ident[:])
        zeros = const.tile([P, 512], BF16, name="zeros")
        nc.vector.memset(zeros[:], 0.0)
        bias_rows = const.tile([P, 256], F32, name="bias_rows")
        nc.vector.memset(bias_rows[:], 0.0)

        bias_raw = const.tile([16, 256], BF16, name="bias_raw")
        nc.scalar.dma_start(out=bias_raw[:], in_=bias.rearrange("(r q) -> r q", q=256))

        x_in = {}
        w_in = {}

        def load_x_pair(pair):
            t = io.tile([P, 2, 2 * K], BF16, name="xin%d" % pair, tag="io")
            for i in range(2):
                bb = 2 * pair + i
                nc.sync.dma_start(out=t[:, i, :], in_=in_data[bb * P : (bb + 1) * P, :])
                x_in[bb] = t[:, i, :]

        def w_tile(J, h):
            if (J, h) not in w_in:
                w_in[(J, h)] = wraw.tile([P, 2, K], BF16, name="w%d_%d" % (J, h), tag="wraw")
            return w_in[(J, h)]

        def w_rows(J, h):
            row0 = h * HALF + J * 256
            return W[row0 : row0 + 256, :].rearrange("(n s) k -> n s k", s=2)

        def load_w(J, h):
            nc.sync.dma_start(out=w_tile(J, h)[:], in_=w_rows(J, h))

        load_x_pair(0)
        for h in (1, 0):
            load_w(0, h)
        load_x_pair(1)
        for h in (1, 0):
            load_w(1, h)
        for h in (1, 0):
            load_w(2, h)
        load_x_pair(2)
        load_x_pair(3)
        for J in range(3, N_J):
            for h in (1, 0):
                load_w(J, h)

        bank_count = [0]

        def next_bank():
            i = bank_count[0] % 4
            bank_count[0] += 1
            return psum.tile([P, 512], F32, name="m%d" % i, tag="m%d" % i)

        r_bank = []
        for bb in range(4):
            t = psum.tile([P, 512], F32, name="rb%d" % bb, tag="rb%d" % bb)
            nc.tensor.matmul(
                out=t[:, 256:512], lhsT=zeros[:, 0:P], rhs=zeros[:, 0:256], start=True, stop=True
            )
            r_bank.append(t)

        idle = psum.tile([P, 512], F32, name="m3", tag="m3")

        def keep_busy(n):
            for i in range(n):
                nc.tensor.matmul(out=idle[:], lhsT=zeros[:, 0:P], rhs=zeros[:], start=True, stop=True)

        spare_count = [0]

        def spare_halves():
            i = spare_count[0] % 4
            spare_count[0] += 2
            return [r_bank[i][:, 0:256], r_bank[i + 1][:, 0:256]]

        def regroup(g_tile, bank, halves):
            words = g_tile[:].bitcast(F32)
            if bank is None:
                for g in range(2):
                    nc.scalar.copy(
                        out=words[:, g * 256 : (g + 1) * 256].rearrange("p (b u) -> p b u", u=2),
                        in_=halves[g].rearrange("p (u b) -> p b u", u=2),
                    )
            else:
                nc.scalar.copy(
                    out=words.rearrange("p (g b u) -> p g b u", g=2, u=2),
                    in_=bank[:].rearrange("p (g u b) -> p g b u", g=2, u=2),
                )

        keep_busy(2)

        nc.vector.tensor_copy(
            out=bias_rows[0:16, :].rearrange("r (s n) -> r s n", s=2),
            in_=bias_raw[0:16, :].rearrange("r (n s) -> r s n", s=2),
        )
        bias_t = next_bank()
        for s in range(2):
            nc.tensor.transpose(
                bias_t[:, s * P : (s + 1) * P], bias_rows[:, s * P : (s + 1) * P], ident[:]
            )
        bias_sb = const.tile([P, 2, 16], F32, name="bias_sb")
        neg_b1 = const.tile([P, 2, 8], F32, name="neg_b1")
        delta = const.tile([P, 2, 8], F32, name="delta")
        nc.scalar.copy(
            out=bias_sb[:], in_=bias_t[:, 0:256].rearrange("p (s r) -> p s r", s=2)[:, :, 0:16]
        )

        def bias_scalars():
            nc.vector.tensor_scalar(
                out=neg_b1[:], in0=bias_sb[:, :, 0:8], scalar1=-1.0, scalar2=None, op0=ALU.mult
            )
            nc.vector.tensor_tensor(
                out=delta[:], in0=bias_sb[:, :, 8:16], in1=bias_sb[:, :, 0:8], op=ALU.subtract
            )

        x_codes = codes.tile([P, 2, B], U32, name="x_codes", align_bytes=256)
        x_scales = codes.tile([P, 2, B], U8, name="x_scales", align_bytes=256)
        w_codes = {}
        w_scales = {}
        for J in range(N_J):
            for h in range(2):
                w_codes[(J, h)] = codes.tile([P, 512], U32, name="wc%d_%d" % (J, h), align_bytes=256)
                w_scales[(J, h)] = codes.tile([P, 512], U8, name="ws%d_%d" % (J, h), align_bytes=256)

        def copy_out(engine, dst, src):
            if engine == "vector":
                nc.vector.tensor_copy(out=dst, in_=src)
            else:
                nc.scalar.copy(out=dst, in_=src)

        x_compact = {}
        x_grouped = {}

        def x_compaction(bb, engine):
            t = stage.tile([P, K], BF16, name="xcmp", tag="xcmp", bufs=4)
            for g in range(2):
                dst = t[:, g * 512 : (g + 1) * 512].rearrange("p (u i e) -> p u i e", u=2, e=2)
                src = x_in[bb][:, g * K : (g + 1) * K].rearrange(
                    "p (i u e two) -> p u i e two", u=2, e=2, two=2
                )[:, :, :, :, 1]
                if engine == "vector":
                    nc.vector.tensor_copy(out=dst, in_=src)
                elif engine == "scalar":
                    nc.scalar.copy(out=dst, in_=src)
                else:
                    nc.gpsimd.tensor_scalar(
                        out=dst, in0=src, scalar1=1.0, scalar2=0.0, op0=ALU.mult, op1=ALU.add
                    )
            x_compact[bb] = t

        def x_transposes(bb, spare=False):
            words = x_compact[bb][:].bitcast(F32)
            bank = None if spare else next_bank()
            halves = spare_halves() if spare else [bank[:, 0:256], bank[:, 256:512]]
            for g in range(2):
                for u in range(2):
                    lo = g * 256 + u * P
                    nc.tensor.transpose(
                        halves[g][:, u * P : (u + 1) * P], words[:, lo : lo + P], ident[:]
                    )
            g_tile = stage.tile([P, K], BF16, name="xg", tag="xg", bufs=4, align_bytes=64)
            regroup(g_tile, bank, halves)
            x_grouped[bb] = g_tile

        def x_quantise(bb):
            for g in range(2):
                nc.vector.quantize_mx(
                    out=x_codes[:, g, bb * P : (bb + 1) * P].bitcast(FP8X4),
                    scales=x_scales[:, g, bb * P : (bb + 1) * P],
                    in_=x_grouped[bb][:, g * 512 : (g + 1) * 512],
                )

        w_ordered = {}
        w_grouped = {}

        def w_order(J, h, s, engine="vector"):
            t = stage.tile([P, K], BF16, name="word", tag="word", bufs=5)
            copy_out(
                engine,
                t[:].bitcast(F32).rearrange("p (g u i) -> p g u i", g=2, u=2),
                w_in[(J, h)][:, s, :].bitcast(F32).rearrange("p (g i u) -> p g u i", g=2, u=2),
            )
            w_ordered[(J, h, s)] = t

        def w_transposes(J, h, s, spare=False):
            words = w_ordered[(J, h, s)][:].bitcast(F32)
            bank = None if spare else next_bank()
            halves = spare_halves() if spare else [bank[:, 0:256], bank[:, 256:512]]
            for g in range(2):
                for u in range(2):
                    lo = g * 256 + u * P
                    nc.tensor.transpose(
                        halves[g][:, u * P : (u + 1) * P], words[:, lo : lo + P], ident[:]
                    )
            g_tile = stage.tile([P, K], BF16, name="wg", tag="wg", bufs=WG_BUFS, align_bytes=64)
            regroup(g_tile, bank, halves)
            w_grouped[(J, h, s)] = g_tile

        def w_quantise(J, h, s):
            nc.vector.quantize_mx(
                out=w_codes[(J, h)][:, s * 256 : (s + 1) * 256].bitcast(FP8X4),
                scales=w_scales[(J, h)][:, s * 256 : (s + 1) * 256],
                in_=w_grouped[(J, h, s)][:],
            )

        def prepare(block, engine="vector"):
            w_order(*block[1:], engine)

        def transpose(block, spare=False):
            if block[0] == "x":
                x_transposes(block[1], spare)
            else:
                w_transposes(*block[1:], spare)

        def quantise(block):
            if block[0] == "x":
                x_quantise(block[1])
            else:
                w_quantise(*block[1:])

        def mx(acc, J, s, h, b0, first, n):
            for g in range(2):
                lo = s * 256 + g * P
                b = slice(b0 + first, b0 + first + n)
                nc.tensor.matmul_mx(
                    out=acc[:, first : first + n],
                    lhsT=w_codes[(J, h)][:, lo : lo + P].bitcast(FP8X4),
                    lhsT_scale=w_scales[(J, h)][:, lo : lo + P],
                    rhs=x_codes[:, g, b].bitcast(FP8X4),
                    rhs_scale=x_scales[:, g, b],
                    start=(g == 0),
                    stop=(g == 1),
                )

        def fold_first(J, nb, s, acc):
            d2 = epi.tile([P, 512], F32, name="d2", tag="d2")
            nc.vector.tensor_scalar(
                out=d2[:, 0:nb], in0=acc[:, 0:nb],
                scalar1=delta[:, s, J : J + 1], scalar2=neg_b1[:, s, J : J + 1],
                op0=ALU.add, op1=ALU.max,
            )
            return d2

        def fold_second(J, nb, s, acc, d2):
            r = epi.tile([P, 512], F32, name="r", tag="r")
            nc.vector.scalar_tensor_tensor(
                out=r[:, 0:nb], in0=acc[:, 0:nb], scalar=neg_b1[:, s, J : J + 1], in1=d2[:, 0:nb],
                op0=ALU.max, op1=ALU.subtract,
            )
            return r

        def r_transposes(b0, nb, r_tiles):
            for bb in range(nb // P):
                for s in range(2):
                    nc.tensor.transpose(
                        r_bank[(b0 // P + bb) % 4][:, s * P : (s + 1) * P],
                        r_tiles[s][:, bb * P : (bb + 1) * P],
                        ident[:],
                    )

        def copy_out_and_store(J, b0, nb, vector_blocks, per_store):
            n_bb = nb // P
            o = io.tile([P, 4, 512], F32, name="o", tag="io")
            view = out2d[b0 : b0 + nb, J * 512 : (J + 1) * 512].rearrange("(bb p) w -> p bb w", p=P)
            for bb in range(n_bb):
                copy_out(
                    "vector" if bb in vector_blocks else "scalar",
                    o[:, bb, :].rearrange("p (n s e) -> p n s e", s=2, e=2),
                    r_bank[(b0 // P + bb) % 4][:].rearrange("p (e s n) -> p n s e", e=2, s=2),
                )
                if bb % per_store == per_store - 1:
                    lo = bb + 1 - per_store
                    nc.sync.dma_start(out=view[:, lo : bb + 1, :], in_=o[:, lo : bb + 1, :])

        rounds = [(0, 0, 256), (0, 256, 256), (1, 0, 512), (2, 0, 512)]
        rounds += [(J, 512, 512) for J in range(3)]
        rounds += [(J, b0, 512) for J in range(3, N_J) for b0 in (0, 512)]
        J, b0, nb = rounds.pop()
        rounds += [(J, b0, 256), (J, b0 + 256, 256)]
        n_rounds = len(rounds)

        def w_blocks(J, h):
            return [("w", J, h, s) for s in range(2)]

        after = {
            0: [("x", 2), ("x", 3)] + w_blocks(1, 1),
            1: w_blocks(1, 0) + w_blocks(2, 1),
            2: w_blocks(2, 0) + [("x", 4), ("x", 5)],
            3: [("x", 6), ("x", 7)],
        }
        for J in range(3, N_J):
            after[2 * J - 2] = w_blocks(J, 1)
            after[2 * J - 1] = w_blocks(J, 0)

        x_compaction(0, "vector")
        x_transposes(0, True)
        x_compaction(1, "vector")
        keep_busy(1)
        x_transposes(1, True)
        for block in w_blocks(0, 1):
            prepare(block)
            transpose(block, True)
        x_quantise(0)
        x_quantise(1)
        for block in w_blocks(0, 0):
            prepare(block)
            transpose(block, True)
        for block in w_blocks(0, 1):
            quantise(block)
        bias_scalars()
        x_compaction(2, "vector")
        for block in w_blocks(0, 0):
            quantise(block)

        waiting = []
        folded = {}
        for i in range(n_rounds):
            J, b0, nb = rounds[i]
            last = i == n_rounds - 1
            if i >= 2:
                copy_out_and_store(
                    *rounds[i - 2],
                    vector_blocks=(3,) if i == n_rounds - 2 else (),
                    per_store=2 if i < n_rounds - 4 else 1,
                )
            acc = {}
            for h in (1, 0):
                for s in range(2):
                    acc[(s, h)] = next_bank()
            for h in (1, 0):
                width = 256 if i == 4 and h == 1 else nb
                for first in range(0, nb, width):
                    for s in range(2):
                        mx(acc[(s, h)], J, s, h, b0, first, width)
            d20 = fold_first(J, nb, 0, acc[(0, 1)])
            d21 = fold_first(J, nb, 1, acc[(1, 1)])
            if i == 0:
                x_compaction(3, "vector")
                for block in w_blocks(1, 1):
                    prepare(block, "scalar")
            r0 = fold_second(J, nb, 0, acc[(0, 0)], d20)
            r1 = fold_second(J, nb, 1, acc[(1, 0)], d21)
            folded[i] = [r0, r1]
            for block in waiting:
                quantise(block)
            waiting = []
            for block in after.get(i, []):
                transpose(block, i == 0 or block[0:3] == ("w", 1, 0))
            if i == 0:
                for block in w_blocks(1, 0):
                    prepare(block, "scalar")
            if i >= 1:
                r_transposes(*rounds[i - 1][1:3], folded[i - 1])
            ahead = [block for block in after.get(i + 1, []) if block[0] == "w" and block[1] >= 2]
            if i == 1:
                x_compaction(4, "scalar")
                x_compaction(5, "vector")
            if i == 2:
                x_compaction(6, "scalar")
                x_compaction(7, "vector")
            if i >= 4:
                for block in ahead:
                    prepare(block)
                waiting = after.get(i, [])
            else:
                for block in after.get(i, []):
                    if block[0:3] in (("w", 2, 1), ("w", 1, 1)):
                        waiting.append(block)
                    else:
                        quantise(block)
                for block in ahead:
                    prepare(block)
        copy_out_and_store(*rounds[n_rounds - 2], vector_blocks=(1,), per_store=1)
        r_transposes(*rounds[n_rounds - 1][1:3], folded[n_rounds - 1])
        copy_out_and_store(*rounds[n_rounds - 1], vector_blocks=(1,), per_store=1)
